import numpy as np
import ml_dtypes


def mxq(x, axis, fmt="e4m3"):
    dtype, down = {"e4m3": (ml_dtypes.float8_e4m3fn, 7), "e5m2": (ml_dtypes.float8_e5m2, 14)}[fmt]
    v = np.moveaxis(np.asarray(x, np.float32).astype(ml_dtypes.bfloat16).astype(np.float64), axis, -1)
    blocks = v.reshape(v.shape[:-1] + (-1, 32))
    amax = np.abs(blocks).max(-1, keepdims=True)
    byte = np.maximum(np.where(amax > 0, np.frexp(amax)[1] - 1 + 127, 0) - down, 1)
    scale = np.exp2(byte - 127.0)
    codes = (blocks / scale).astype(np.float32).astype(dtype).astype(np.float64)
    return np.moveaxis((codes * scale).reshape(v.shape), -1, axis)


WIDE = False


def mx_kscale(k):
    if not WIDE:
        return np.ones(k)
    levels = np.array([10, -10, 5, -5, 0])
    a = np.random.permutation(np.resize(levels, k // 512 * 4)).reshape(k // 512, 4)
    idx = np.arange(k)
    return np.exp2(a[idx // 512, idx % 128 // 32])


BF16 = ml_dtypes.bfloat16


def bf(x):
    return np.asarray(x, np.float32).astype(BF16)


def f64(x):
    return np.asarray(x).astype(np.float64)


E2M1 = np.array([0.0, 0.5, 1.0, 1.5, 2.0, 3.0, 4.0, 6.0, -0.0, -0.5, -1.0, -1.5, -2.0, -3.0, -4.0, -6.0])


def pack_weight(w, fmt):
    k, n = w.shape
    w = f64(bf(w)).reshape(k // 32, 32, n)
    amax = np.abs(w).max(1)
    if fmt == "e4m3":
        byte = np.frexp(amax)[1] - 1 + 127 - 7
    else:
        mant, ex = np.frexp(amax / 6.0)
        byte = np.where(mant > 0.5, ex, ex - 1) + 127
    byte = np.clip(np.where(amax > 0, byte, 1), 1, 254)
    scaled = (w * np.exp2(127.0 - byte)[:, None, :]).reshape(k, n).astype(np.float32)
    by_word = np.ascontiguousarray(scaled.reshape(k // 512, 128, 4, n).transpose(0, 1, 3, 2))
    if fmt == "e4m3":
        words = by_word.astype(ml_dtypes.float8_e4m3fn).view(np.uint8)
    else:
        c = by_word.astype(ml_dtypes.float4_e2m1fn).view(np.uint8) & 0xF
        words = c[..., 0::2] | (c[..., 1::2] << 4)
    return np.ascontiguousarray(words), np.ascontiguousarray(byte.astype(np.uint8).reshape(k // 512, 16, n))


def unpack_weight(words, scales, fmt):
    g, p, n, _ = words.shape
    if fmt == "e4m3":
        vals = np.ascontiguousarray(words).view(ml_dtypes.float8_e4m3fn).astype(np.float64)
    else:
        nib = np.empty((g, p, n, 4), np.uint8)
        nib[..., 0::2] = words & 0xF
        nib[..., 1::2] = words >> 4
        vals = E2M1[nib]
    vals = vals * np.repeat(np.exp2(scales.astype(np.float64) - 127.0), 8, axis=1)[..., None]
    return vals.transpose(0, 1, 3, 2).reshape(g * 512, n)

def pack4(w):
    words, scales = pack_weight(w, "e2m1")
    return words.reshape(words.shape[0], 128, -1), scales


def unpack4(words, scales):
    return unpack_weight(words.reshape(words.shape[0], 128, -1, 2), scales, "e2m1")


B, S, HID, NH, HD, RD, RATIO = 4, 4096, 512, 2, 64, 32, 4
THETA = 10000.0
HALF = RD // 2


def rope_tables(positions):
    inv_freq = 1.0 / THETA ** (np.arange(HALF) / HALF)
    ang = positions[:, None] * inv_freq[None, :]
    return np.cos(ang), np.sin(ang)


def rope_interleaved(x, cos, sin):
    nope, rope = x[..., :-RD], x[..., -RD:]
    pr = rope.reshape(rope.shape[:-1] + (HALF, 2))
    a, b = pr[..., 0], pr[..., 1]
    new = np.stack([a * cos - b * sin, a * sin + b * cos], axis=-1).reshape(rope.shape)
    return np.concatenate([nope, new], axis=-1)


def setup_inputs():
    s = mx_kscale(HID)
    hidden = bf(np.random.standard_normal((B, S, HID)) * s)
    wq_words, wq_scales = pack4(np.random.standard_normal((HID, NH * HD)) / np.sqrt(HID) / s[:, None])
    return {"hidden": hidden,
            "wq_words": wq_words,
            "wq_scales": wq_scales}


def reference(hidden, wq_words, wq_scales):
    q = mxq(f64(hidden), 2, "e4m3") @ unpack4(wq_words, wq_scales)
    q = q.reshape(B, S, NH, HD).transpose(0, 2, 1, 3)
    cq, sq = rope_tables(np.arange(S))
    return rope_interleaved(q, cq, sq)

@@ -1,0 +1,232 @@
+from contextlib import ExitStack
+
+import concourse.mybir as mybir
+from concourse.masks import make_identity
+
+F32 = mybir.dt.float32
+BF16 = mybir.dt.bfloat16
+I32 = mybir.dt.int32
+U32 = mybir.dt.uint32
+U8 = mybir.dt.uint8
+FP8X4 = mybir.dt.float8_e4m3fn_x4
+FP4X4 = mybir.dt.float4_e2m1fn_x4
+ALU = mybir.AluOpType
+SIN = mybir.ActivationFunctionType.Sin
+
+BATCH, SEQ, HID, HEADS, HEAD_DIM, ROPE_DIM = 4, 4096, 512, 2, 64, 32
+FEATURES = HEADS * HEAD_DIM
+PLAIN_DIM = HEAD_DIM - ROPE_DIM
+PAIRS = ROPE_DIM // 2
+THETA = 10000.0
+TWO_PI = 6.283185307179586
+
+P = 128
+TOKENS_PER_PARTITION = SEQ // P
+WORDS = HID // 2
+CHUNK = 8
+T_BANK = 2
+Y_BANK = 4
+ROUND_MAGIC = 12582912.0
+
+FLOPS = 2 * BATCH * SEQ * HID * FEATURES
+
+
+def split_turns_per_position(j):
+    turns = THETA ** (-j / PAIRS) / TWO_PI
+    scale = 1.0
+    while turns * scale < 2048.0:
+        scale *= 2.0
+    coarse = round(turns * scale) / scale
+    return coarse, turns - coarse
+
+
+def tile_deepseekv4attention_pb_t_kernel(tc, hidden, wq_words, wq_scales, out):
+    nc = tc.nc
+    chunks = [(b, i0) for b in range(BATCH) for i0 in range(0, TOKENS_PER_PARTITION, CHUNK)]
+    n_chunks = len(chunks)
+
+    with ExitStack() as ctx:
+        consts = ctx.enter_context(tc.tile_pool(name="consts", bufs=1))
+        x_pool = ctx.enter_context(tc.tile_pool(name="x", bufs=n_chunks))
+        mx_pool = ctx.enter_context(tc.tile_pool(name="mx", bufs=2))
+        rope_pool = ctx.enter_context(tc.tile_pool(name="rope", bufs=2))
+        res_pool = ctx.enter_context(tc.tile_pool(name="res", bufs=8))
+        t_psum = ctx.enter_context(tc.psum_pool(name="t_psum", bufs=4))
+        y_psum = ctx.enter_context(tc.psum_pool(name="y_psum", bufs=4))
+        ctx.enter_context(tc.manual_schedule())
+
+        w_words = consts.tile([P, 2 * FEATURES], U8, align_bytes=64)
+        w_scales = consts.tile([P, FEATURES], U8, align_bytes=64)
+        nc.vector.memset(w_scales[:].bitcast(I32), 0)
+
+        x_tiles = []
+        for c, (b, i0) in enumerate(chunks):
+            x = x_pool.tile([P, CHUNK, HID], BF16)
+            rows = hidden[b].rearrange("(p i) k -> p i k", i=TOKENS_PER_PARTITION)
+            piece = T_BANK if c == 0 else CHUNK
+            for a0 in range(0, CHUNK, piece):
+                nc.sync.dma_start(out=x[:, a0 : a0 + piece, :], in_=rows[:, i0 + a0 : i0 + a0 + piece, :])
+            x_tiles.append(x)
+            if c == 0:
+                nc.sync.dma_start(out=w_words[:].bitcast(I32), in_=wq_words[0].bitcast(I32))
+                for quadrant in range(4):
+                    nc.sync.dma_start(
+                        out=w_scales[32 * quadrant : 32 * quadrant + 4, :].bitcast(I32),
+                        in_=wq_scales[0, 4 * quadrant : 4 * quadrant + 4, :].bitcast(I32),
+                    )
+
+        position_int = consts.tile([P, TOKENS_PER_PARTITION], I32)
+        nc.gpsimd.iota(
+            position_int[:],
+            pattern=[[1, TOKENS_PER_PARTITION]],
+            base=0,
+            channel_multiplier=TOKENS_PER_PARTITION,
+        )
+        identity = consts.tile([P, P], F32)
+        make_identity(nc, identity[:])
+
+        zero = consts.tile([P, 1], F32)
+        nc.vector.memset(zero[:], 0.0)
+        warm = consts.tile([P, 1], F32)
+        nc.scalar.activation(out=warm[:], in_=zero[:], func=SIN)
+
+        position = consts.tile([P, TOKENS_PER_PARTITION], F32)
+        nc.vector.tensor_copy(out=position[:], in_=position_int[:])
+        splits = [split_turns_per_position(j) for j in range(PAIRS)]
+        turns = consts.tile([P, PAIRS, TOKENS_PER_PARTITION], F32)
+        whole = consts.tile([P, PAIRS, TOKENS_PER_PARTITION], F32)
+        for j in range(PAIRS):
+            nc.vector.tensor_scalar(
+                out=turns[:, j, :], in0=position[:], scalar1=splits[j][0], scalar2=None, op0=ALU.mult
+            )
+        nc.vector.tensor_scalar(
+            out=whole[:], in0=turns[:], scalar1=ROUND_MAGIC, scalar2=ROUND_MAGIC, op0=ALU.add, op1=ALU.subtract
+        )
+        nc.vector.tensor_tensor(out=turns[:], in0=turns[:], in1=whole[:], op=ALU.subtract)
+        for j in range(PAIRS):
+            nc.vector.scalar_tensor_tensor(
+                out=turns[:, j, :],
+                in0=position[:],
+                scalar=splits[j][1],
+                in1=turns[:, j, :],
+                op0=ALU.mult,
+                op1=ALU.add,
+            )
+        nc.vector.tensor_scalar(
+            out=whole[:], in0=turns[:], scalar1=ROUND_MAGIC, scalar2=ROUND_MAGIC, op0=ALU.add, op1=ALU.subtract
+        )
+        angle = consts.tile([P, TOKENS_PER_PARTITION, PAIRS], F32)
+        nc.vector.tensor_tensor(
+            out=angle[:],
+            in0=turns[:].rearrange("p j i -> p i j"),
+            in1=whole[:].rearrange("p j i -> p i j"),
+            op=ALU.subtract,
+        )
+        quarter_less_angle = consts.tile([P, TOKENS_PER_PARTITION, PAIRS], F32)
+        nc.vector.scalar_tensor_tensor(
+            out=quarter_less_angle[:], in0=angle[:], scalar=-1.0, in1=angle[:], op0=ALU.mult, op1=ALU.min
+        )
+        nc.vector.tensor_scalar(
+            out=quarter_less_angle[:], in0=quarter_less_angle[:], scalar1=0.25, scalar2=None, op0=ALU.add
+        )
+        table = consts.tile([P, TOKENS_PER_PARTITION, 3, PAIRS], F32)
+
+        def fill_table():
+            nc.scalar.activation(out=table[:, :, 0, :], in_=angle[:], func=SIN, scale=-TWO_PI)
+            nc.scalar.activation(out=table[:, :, 1, :], in_=quarter_less_angle[:], func=SIN, scale=TWO_PI)
+            nc.scalar.activation(out=table[:, :, 2, :], in_=angle[:], func=SIN, scale=TWO_PI)
+
+        grouped_of = {}
+        y_of = {}
+
+        def transpose(c):
+            x_words = x_tiles[c][:].rearrange("p a k -> p (a k)").bitcast(F32)
+            grouped = mx_pool.tile([P, CHUNK * P * 4], BF16, align_bytes=64)
+            grouped_words = grouped[:].bitcast(F32).rearrange("p (a n u) -> p a n u", n=P, u=2)
+            for a0 in range(0, CHUNK, T_BANK):
+                flipped = t_psum.tile([P, T_BANK, 2, P], F32)
+                for a in range(T_BANK):
+                    first_word = (a0 + a) * WORDS
+                    for u in range(2):
+                        nc.tensor.transpose(
+                            flipped[:, a, u, :],
+                            x_words[:, first_word + u : first_word + WORDS : 2],
+                            identity[:],
+                        )
+                nc.scalar.copy(
+                    out=grouped_words[:, a0 : a0 + T_BANK, :, :],
+                    in_=flipped[:].rearrange("p a u n -> p a n u"),
+                )
+            grouped_of[c] = grouped
+
+        def project(c):
+            codes = mx_pool.tile([P, CHUNK * P], U32, align_bytes=64)
+            scales = mx_pool.tile([P, CHUNK * P], U8, align_bytes=64)
+            y_of[c] = []
+            for a0 in range(0, CHUNK, Y_BANK):
+                tokens = slice(a0 * P, (a0 + Y_BANK) * P)
+                nc.vector.quantize_mx(
+                    out=codes[:, tokens].bitcast(FP8X4),
+                    scales=scales[:, tokens],
+                    in_=grouped_of[c][:, 4 * a0 * P : 4 * (a0 + Y_BANK) * P],
+                )
+            for a0 in range(0, CHUNK, Y_BANK):
+                y = y_psum.tile([P, Y_BANK, FEATURES], F32)
+                for a in range(Y_BANK):
+                    tokens = slice((a0 + a) * P, (a0 + a + 1) * P)
+                    nc.tensor.matmul_mx(
+                        out=y[:, a, :],
+                        lhsT=codes[:, tokens].bitcast(FP8X4),
+                        lhsT_scale=scales[:, tokens],
+                        rhs=w_words[:].bitcast(FP4X4),
+                        rhs_scale=w_scales[:],
+                        start=True,
+                        stop=True,
+                    )
+                y_of[c].append(y)
+
+        def rotate(c):
+            b, i0 = chunks[c]
+            from_first = rope_pool.tile([P, CHUNK, HEADS, 2, PAIRS], F32)
+            from_second = rope_pool.tile([P, CHUNK, HEADS, 2, PAIRS], F32)
+            res = res_pool.tile([P, HEADS, CHUNK, HEAD_DIM], F32)
+            shape = [P, Y_BANK, HEADS, 2, PAIRS]
+            for bank, a0 in enumerate(range(0, CHUNK, Y_BANK)):
+                y = y_of[c][bank][:].rearrange("p a (h d) -> p a h d", h=HEADS)
+                rows = table[:, i0 + a0 : i0 + a0 + Y_BANK, :, :]
+                nc.vector.tensor_tensor(
+                    out=from_first[:, a0 : a0 + Y_BANK],
+                    in0=y[:, :, :, PLAIN_DIM:HEAD_DIM:2].unsqueeze(3).to_broadcast(shape),
+                    in1=rows[:, :, 1:3, :].unsqueeze(2).to_broadcast(shape),
+                    op=ALU.mult,
+                )
+                nc.vector.tensor_tensor(
+                    out=from_second[:, a0 : a0 + Y_BANK],
+                    in0=y[:, :, :, PLAIN_DIM + 1 : HEAD_DIM : 2].unsqueeze(3).to_broadcast(shape),
+                    in1=rows[:, :, 0:2, :].unsqueeze(2).to_broadcast(shape),
+                    op=ALU.mult,
+                )
+                nc.scalar.copy(
+                    out=res[:, :, a0 : a0 + Y_BANK, 0:PLAIN_DIM].rearrange("p h a d -> p a h d"),
+                    in_=y[:, :, :, 0:PLAIN_DIM],
+                )
+            nc.vector.tensor_tensor(
+                out=res[:, :, :, PLAIN_DIM:HEAD_DIM].rearrange("p h a (j e) -> p a h j e", e=2),
+                in0=from_first[:].rearrange("p a h e j -> p a h j e"),
+                in1=from_second[:].rearrange("p a h e j -> p a h j e"),
+                op=ALU.add,
+            )
+            rows_out = out[b].rearrange("h (p i) d -> p h i d", i=TOKENS_PER_PARTITION)
+            nc.gpsimd.dma_start(out=rows_out[:, :, i0 : i0 + CHUNK, :], in_=res[:])
+
+        transpose(0)
+        fill_table()
+        transpose(1)
+        project(0)
+        for c in range(2, n_chunks):
+            transpose(c)
+            project(c - 1)
+            rotate(c - 2)
+        project(n_chunks - 1)
+        rotate(n_chunks - 2)
+        rotate(n_chunks - 1)

@@ -24,8 +24,8 @@ P = 128
 TOKENS_PER_PARTITION = SEQ // P
 WORDS = HID // 2
 CHUNK = 8
+GROUP = 4
 T_BANK = 2
-Y_BANK = 4
 ROUND_MAGIC = 12582912.0
 
 FLOPS = 2 * BATCH * SEQ * HID * FEATURES
@@ -44,12 +44,13 @@ def tile_deepseekv4attention_pb_t_kernel(tc, hidden, wq_words, wq_scales, out):
     nc = tc.nc
     chunks = [(b, i0) for b in range(BATCH) for i0 in range(0, TOKENS_PER_PARTITION, CHUNK)]
     n_chunks = len(chunks)
+    n_groups = n_chunks * CHUNK // GROUP
 
     with ExitStack() as ctx:
         consts = ctx.enter_context(tc.tile_pool(name="consts", bufs=1))
         x_pool = ctx.enter_context(tc.tile_pool(name="x", bufs=n_chunks))
-        mx_pool = ctx.enter_context(tc.tile_pool(name="mx", bufs=2))
-        rope_pool = ctx.enter_context(tc.tile_pool(name="rope", bufs=2))
+        mx_pool = ctx.enter_context(tc.tile_pool(name="mx", bufs=3))
+        rope_pool = ctx.enter_context(tc.tile_pool(name="rope", bufs=3))
         res_pool = ctx.enter_context(tc.tile_pool(name="res", bufs=8))
         t_psum = ctx.enter_context(tc.psum_pool(name="t_psum", bufs=4))
         y_psum = ctx.enter_context(tc.psum_pool(name="y_psum", bufs=4))
@@ -138,15 +139,17 @@ def tile_deepseekv4attention_pb_t_kernel(tc, hidden, wq_words, wq_scales, out):
 
         grouped_of = {}
         y_of = {}
+        res_of = {}
 
-        def transpose(c):
-            x_words = x_tiles[c][:].rearrange("p a k -> p (a k)").bitcast(F32)
-            grouped = mx_pool.tile([P, CHUNK * P * 4], BF16, align_bytes=64)
+        def transpose(g):
+            x_words = x_tiles[g * GROUP // CHUNK][:].rearrange("p a k -> p (a k)").bitcast(F32)
+            first_tile = g * GROUP % CHUNK
+            grouped = mx_pool.tile([P, GROUP * P * 4], BF16, align_bytes=64)
             grouped_words = grouped[:].bitcast(F32).rearrange("p (a n u) -> p a n u", n=P, u=2)
-            for a0 in range(0, CHUNK, T_BANK):
+            for a0 in range(0, GROUP, T_BANK):
                 flipped = t_psum.tile([P, T_BANK, 2, P], F32)
                 for a in range(T_BANK):
-                    first_word = (a0 + a) * WORDS
+                    first_word = (first_tile + a0 + a) * WORDS
                     for u in range(2):
                         nc.tensor.transpose(
                             flipped[:, a, u, :],
@@ -157,76 +160,72 @@ def tile_deepseekv4attention_pb_t_kernel(tc, hidden, wq_words, wq_scales, out):
                     out=grouped_words[:, a0 : a0 + T_BANK, :, :],
                     in_=flipped[:].rearrange("p a u n -> p a n u"),
                 )
-            grouped_of[c] = grouped
+            grouped_of[g] = grouped
 
-        def project(c):
-            codes = mx_pool.tile([P, CHUNK * P], U32, align_bytes=64)
-            scales = mx_pool.tile([P, CHUNK * P], U8, align_bytes=64)
-            y_of[c] = []
-            for a0 in range(0, CHUNK, Y_BANK):
-                tokens = slice(a0 * P, (a0 + Y_BANK) * P)
-                nc.vector.quantize_mx(
-                    out=codes[:, tokens].bitcast(FP8X4),
-                    scales=scales[:, tokens],
-                    in_=grouped_of[c][:, 4 * a0 * P : 4 * (a0 + Y_BANK) * P],
+        def project(g):
+            codes = mx_pool.tile([P, GROUP * P], U32, align_bytes=64)
+            scales = mx_pool.tile([P, GROUP * P], U8, align_bytes=64)
+            nc.vector.quantize_mx(out=codes[:].bitcast(FP8X4), scales=scales[:], in_=grouped_of[g][:])
+            y = y_psum.tile([P, GROUP, FEATURES], F32)
+            for a in range(GROUP):
+                tokens = slice(a * P, (a + 1) * P)
+                nc.tensor.matmul_mx(
+                    out=y[:, a, :],
+                    lhsT=codes[:, tokens].bitcast(FP8X4),
+                    lhsT_scale=scales[:, tokens],
+                    rhs=w_words[:].bitcast(FP4X4),
+                    rhs_scale=w_scales[:],
+                    start=True,
+                    stop=True,
                 )
-            for a0 in range(0, CHUNK, Y_BANK):
-                y = y_psum.tile([P, Y_BANK, FEATURES], F32)
-                for a in range(Y_BANK):
-                    tokens = slice((a0 + a) * P, (a0 + a + 1) * P)
-                    nc.tensor.matmul_mx(
-                        out=y[:, a, :],
-                        lhsT=codes[:, tokens].bitcast(FP8X4),
-                        lhsT_scale=scales[:, tokens],
-                        rhs=w_words[:].bitcast(FP4X4),
-                        rhs_scale=w_scales[:],
-                        start=True,
-                        stop=True,
-                    )
-                y_of[c].append(y)
+            y_of[g] = y
 
-        def rotate(c):
+        def rotate(g):
+            c = g * GROUP // CHUNK
+            a0 = g * GROUP % CHUNK
             b, i0 = chunks[c]
-            from_first = rope_pool.tile([P, CHUNK, HEADS, 2, PAIRS], F32)
-            from_second = rope_pool.tile([P, CHUNK, HEADS, 2, PAIRS], F32)
-            res = res_pool.tile([P, HEADS, CHUNK, HEAD_DIM], F32)
-            shape = [P, Y_BANK, HEADS, 2, PAIRS]
-            for bank, a0 in enumerate(range(0, CHUNK, Y_BANK)):
-                y = y_of[c][bank][:].rearrange("p a (h d) -> p a h d", h=HEADS)
-                rows = table[:, i0 + a0 : i0 + a0 + Y_BANK, :, :]
-                nc.vector.tensor_tensor(
-                    out=from_first[:, a0 : a0 + Y_BANK],
-                    in0=y[:, :, :, PLAIN_DIM:HEAD_DIM:2].unsqueeze(3).to_broadcast(shape),
-                    in1=rows[:, :, 1:3, :].unsqueeze(2).to_broadcast(shape),
-                    op=ALU.mult,
-                )
-                nc.vector.tensor_tensor(
-                    out=from_second[:, a0 : a0 + Y_BANK],
-                    in0=y[:, :, :, PLAIN_DIM + 1 : HEAD_DIM : 2].unsqueeze(3).to_broadcast(shape),
-                    in1=rows[:, :, 0:2, :].unsqueeze(2).to_broadcast(shape),
-                    op=ALU.mult,
-                )
-                nc.scalar.copy(
-                    out=res[:, :, a0 : a0 + Y_BANK, 0:PLAIN_DIM].rearrange("p h a d -> p a h d"),
-                    in_=y[:, :, :, 0:PLAIN_DIM],
-                )
+            if a0 == 0:
+                res_of[c] = res_pool.tile([P, HEADS, CHUNK, HEAD_DIM], F32, name="res")
+            res = res_of[c][:, :, a0 : a0 + GROUP, :]
+            from_first = rope_pool.tile([P, GROUP, HEADS, 2, PAIRS], F32)
+            from_second = rope_pool.tile([P, GROUP, HEADS, 2, PAIRS], F32)
+            shape = [P, GROUP, HEADS, 2, PAIRS]
+            y = y_of[g][:].rearrange("p a (h d) -> p a h d", h=HEADS)
+            rows = table[:, i0 + a0 : i0 + a0 + GROUP, :, :]
+            nc.vector.tensor_tensor(
+                out=from_first[:],
+                in0=y[:, :, :, PLAIN_DIM:HEAD_DIM:2].unsqueeze(3).to_broadcast(shape),
+                in1=rows[:, :, 1:3, :].unsqueeze(2).to_broadcast(shape),
+                op=ALU.mult,
+            )
+            nc.vector.tensor_tensor(
+                out=from_second[:],
+                in0=y[:, :, :, PLAIN_DIM + 1 : HEAD_DIM : 2].unsqueeze(3).to_broadcast(shape),
+                in1=rows[:, :, 0:2, :].unsqueeze(2).to_broadcast(shape),
+                op=ALU.mult,
+            )
+            nc.scalar.copy(
+                out=res[:, :, :, 0:PLAIN_DIM].rearrange("p h a d -> p a h d"),
+                in_=y[:, :, :, 0:PLAIN_DIM],
+            )
             nc.vector.tensor_tensor(
                 out=res[:, :, :, PLAIN_DIM:HEAD_DIM].rearrange("p h a (j e) -> p a h j e", e=2),
                 in0=from_first[:].rearrange("p a h e j -> p a h j e"),
                 in1=from_second[:].rearrange("p a h e j -> p a h j e"),
                 op=ALU.add,
             )
-            rows_out = out[b].rearrange("h (p i) d -> p h i d", i=TOKENS_PER_PARTITION)
-            nc.gpsimd.dma_start(out=rows_out[:, :, i0 : i0 + CHUNK, :], in_=res[:])
+            if a0 + GROUP == CHUNK:
+                rows_out = out[b].rearrange("h (p i) d -> p h i d", i=TOKENS_PER_PARTITION)
+                nc.gpsimd.dma_start(out=rows_out[:, :, i0 : i0 + CHUNK, :], in_=res_of[c][:])
 
         transpose(0)
-        fill_table()
         transpose(1)
         project(0)
-        for c in range(2, n_chunks):
-            transpose(c)
-            project(c - 1)
-            rotate(c - 2)
-        project(n_chunks - 1)
-        rotate(n_chunks - 2)
-        rotate(n_chunks - 1)
+        fill_table()
+        for g in range(2, n_groups):
+            transpose(g)
+            project(g - 1)
+            rotate(g - 2)
+        project(n_groups - 1)
+        rotate(n_groups - 2)
+        rotate(n_groups - 1)

@@ -23,9 +23,10 @@ TWO_PI = 6.283185307179586
 P = 128
 TOKENS_PER_PARTITION = SEQ // P
 WORDS = HID // 2
-CHUNK = 8
 GROUP = 4
 T_BANK = 2
+CHUNK = 8
+RUN = 2
 ROUND_MAGIC = 12582912.0
 
 FLOPS = 2 * BATCH * SEQ * HID * FEATURES
@@ -42,16 +43,15 @@ def split_turns_per_position(j):
 
 def tile_deepseekv4attention_pb_t_kernel(tc, hidden, wq_words, wq_scales, out):
     nc = tc.nc
-    chunks = [(b, i0) for b in range(BATCH) for i0 in range(0, TOKENS_PER_PARTITION, CHUNK)]
-    n_chunks = len(chunks)
-    n_groups = n_chunks * CHUNK // GROUP
+    groups = [(b, i0) for b in range(BATCH) for i0 in range(0, TOKENS_PER_PARTITION, GROUP)]
+    n_groups = len(groups)
 
     with ExitStack() as ctx:
         consts = ctx.enter_context(tc.tile_pool(name="consts", bufs=1))
-        x_pool = ctx.enter_context(tc.tile_pool(name="x", bufs=n_chunks))
-        mx_pool = ctx.enter_context(tc.tile_pool(name="mx", bufs=3))
-        rope_pool = ctx.enter_context(tc.tile_pool(name="rope", bufs=3))
-        res_pool = ctx.enter_context(tc.tile_pool(name="res", bufs=8))
+        x_pool = ctx.enter_context(tc.tile_pool(name="x", bufs=n_groups))
+        mx_pool = ctx.enter_context(tc.tile_pool(name="mx", bufs=4))
+        rope_pool = ctx.enter_context(tc.tile_pool(name="rope", bufs=4))
+        res_pool = ctx.enter_context(tc.tile_pool(name="res", bufs=12))
         t_psum = ctx.enter_context(tc.psum_pool(name="t_psum", bufs=4))
         y_psum = ctx.enter_context(tc.psum_pool(name="y_psum", bufs=4))
         ctx.enter_context(tc.manual_schedule())
@@ -60,21 +60,24 @@ def tile_deepseekv4attention_pb_t_kernel(tc, hidden, wq_words, wq_scales, out):
         w_scales = consts.tile([P, FEATURES], U8, align_bytes=64)
         nc.vector.memset(w_scales[:].bitcast(I32), 0)
 
+        def load_w():
+            nc.sync.dma_start(out=w_words[:].bitcast(I32), in_=wq_words[0].bitcast(I32))
+            for quadrant in range(4):
+                nc.sync.dma_start(
+                    out=w_scales[32 * quadrant : 32 * quadrant + 4, :].bitcast(I32),
+                    in_=wq_scales[0, 4 * quadrant : 4 * quadrant + 4, :].bitcast(I32),
+                )
+
         x_tiles = []
-        for c, (b, i0) in enumerate(chunks):
-            x = x_pool.tile([P, CHUNK, HID], BF16)
+        for g, (b, i0) in enumerate(groups):
+            x = x_pool.tile([P, GROUP, HID], BF16)
             rows = hidden[b].rearrange("(p i) k -> p i k", i=TOKENS_PER_PARTITION)
-            piece = T_BANK if c == 0 else CHUNK
-            for a0 in range(0, CHUNK, piece):
+            piece = T_BANK if g < RUN else GROUP
+            for a0 in range(0, GROUP, piece):
                 nc.sync.dma_start(out=x[:, a0 : a0 + piece, :], in_=rows[:, i0 + a0 : i0 + a0 + piece, :])
             x_tiles.append(x)
-            if c == 0:
-                nc.sync.dma_start(out=w_words[:].bitcast(I32), in_=wq_words[0].bitcast(I32))
-                for quadrant in range(4):
-                    nc.sync.dma_start(
-                        out=w_scales[32 * quadrant : 32 * quadrant + 4, :].bitcast(I32),
-                        in_=wq_scales[0, 4 * quadrant : 4 * quadrant + 4, :].bitcast(I32),
-                    )
+            if g == 2 * RUN - 1:
+                load_w()
 
         position_int = consts.tile([P, TOKENS_PER_PARTITION], I32)
         nc.gpsimd.iota(
@@ -116,40 +119,40 @@ def tile_deepseekv4attention_pb_t_kernel(tc, hidden, wq_words, wq_scales, out):
         nc.vector.tensor_scalar(
             out=whole[:], in0=turns[:], scalar1=ROUND_MAGIC, scalar2=ROUND_MAGIC, op0=ALU.add, op1=ALU.subtract
         )
-        angle = consts.tile([P, TOKENS_PER_PARTITION, PAIRS], F32)
+        sin_of = consts.tile([P, 3, TOKENS_PER_PARTITION, PAIRS], F32)
         nc.vector.tensor_tensor(
-            out=angle[:],
+            out=sin_of[:, 2],
             in0=turns[:].rearrange("p j i -> p i j"),
             in1=whole[:].rearrange("p j i -> p i j"),
             op=ALU.subtract,
         )
-        quarter_less_angle = consts.tile([P, TOKENS_PER_PARTITION, PAIRS], F32)
-        nc.vector.scalar_tensor_tensor(
-            out=quarter_less_angle[:], in0=angle[:], scalar=-1.0, in1=angle[:], op0=ALU.mult, op1=ALU.min
-        )
-        nc.vector.tensor_scalar(
-            out=quarter_less_angle[:], in0=quarter_less_angle[:], scalar1=0.25, scalar2=None, op0=ALU.add
-        )
-        table = consts.tile([P, TOKENS_PER_PARTITION, 3, PAIRS], F32)
+        nc.vector.tensor_scalar(out=sin_of[:, 0], in0=sin_of[:, 2], scalar1=-1.0, scalar2=None, op0=ALU.mult)
+        nc.vector.tensor_tensor(out=sin_of[:, 1], in0=sin_of[:, 0], in1=sin_of[:, 2], op=ALU.min)
+        nc.vector.tensor_scalar(out=sin_of[:, 1], in0=sin_of[:, 1], scalar1=0.25, scalar2=None, op0=ALU.add)
+        first_factors = consts.tile([P, TOKENS_PER_PARTITION, PAIRS, 2], F32)
+        second_factors = consts.tile([P, TOKENS_PER_PARTITION, PAIRS, 2], F32)
 
-        def fill_table():
-            nc.scalar.activation(out=table[:, :, 0, :], in_=angle[:], func=SIN, scale=-TWO_PI)
-            nc.scalar.activation(out=table[:, :, 1, :], in_=quarter_less_angle[:], func=SIN, scale=TWO_PI)
-            nc.scalar.activation(out=table[:, :, 2, :], in_=angle[:], func=SIN, scale=TWO_PI)
+        def fill_tables():
+            nc.scalar.activation(
+                out=first_factors[:], in_=sin_of[:, 1:3].rearrange("p e i j -> p i j e"), func=SIN, scale=TWO_PI
+            )
+            nc.scalar.activation(
+                out=second_factors[:], in_=sin_of[:, 0:2].rearrange("p e i j -> p i j e"), func=SIN, scale=TWO_PI
+            )
 
         grouped_of = {}
+        mx_of = {}
         y_of = {}
         res_of = {}
 
         def transpose(g):
-            x_words = x_tiles[g * GROUP // CHUNK][:].rearrange("p a k -> p (a k)").bitcast(F32)
-            first_tile = g * GROUP % CHUNK
+            x_words = x_tiles[g][:].rearrange("p a k -> p (a k)").bitcast(F32)
             grouped = mx_pool.tile([P, GROUP * P * 4], BF16, align_bytes=64)
             grouped_words = grouped[:].bitcast(F32).rearrange("p (a n u) -> p a n u", n=P, u=2)
             for a0 in range(0, GROUP, T_BANK):
                 flipped = t_psum.tile([P, T_BANK, 2, P], F32)
                 for a in range(T_BANK):
-                    first_word = (first_tile + a0 + a) * WORDS
+                    first_word = (a0 + a) * WORDS
                     for u in range(2):
                         nc.tensor.transpose(
                             flipped[:, a, u, :],
@@ -162,10 +165,14 @@ def tile_deepseekv4attention_pb_t_kernel(tc, hidden, wq_words, wq_scales, out):
                 )
             grouped_of[g] = grouped
 
-        def project(g):
+        def quantise(g):
             codes = mx_pool.tile([P, GROUP * P], U32, align_bytes=64)
             scales = mx_pool.tile([P, GROUP * P], U8, align_bytes=64)
             nc.vector.quantize_mx(out=codes[:].bitcast(FP8X4), scales=scales[:], in_=grouped_of[g][:])
+            mx_of[g] = (codes, scales)
+
+        def multiply(g):
+            codes, scales = mx_of[g]
             y = y_psum.tile([P, GROUP, FEATURES], F32)
             for a in range(GROUP):
                 tokens = slice(a * P, (a + 1) * P)
@@ -181,51 +188,51 @@ def tile_deepseekv4attention_pb_t_kernel(tc, hidden, wq_words, wq_scales, out):
             y_of[g] = y
 
         def rotate(g):
+            b, i0 = groups[g]
             c = g * GROUP // CHUNK
             a0 = g * GROUP % CHUNK
-            b, i0 = chunks[c]
             if a0 == 0:
                 res_of[c] = res_pool.tile([P, HEADS, CHUNK, HEAD_DIM], F32, name="res")
-            res = res_of[c][:, :, a0 : a0 + GROUP, :]
-            from_first = rope_pool.tile([P, GROUP, HEADS, 2, PAIRS], F32)
-            from_second = rope_pool.tile([P, GROUP, HEADS, 2, PAIRS], F32)
-            shape = [P, GROUP, HEADS, 2, PAIRS]
+            res = res_of[c][:, :, a0 : a0 + GROUP, :].rearrange("p h a d -> p a h d")
             y = y_of[g][:].rearrange("p a (h d) -> p a h d", h=HEADS)
-            rows = table[:, i0 + a0 : i0 + a0 + GROUP, :, :]
+            from_first = rope_pool.tile([P, GROUP, HEADS, PAIRS, 2], F32)
+            from_second = rope_pool.tile([P, GROUP, HEADS, PAIRS, 2], F32)
+            shape = [P, GROUP, HEADS, PAIRS, 2]
             nc.vector.tensor_tensor(
                 out=from_first[:],
-                in0=y[:, :, :, PLAIN_DIM:HEAD_DIM:2].unsqueeze(3).to_broadcast(shape),
-                in1=rows[:, :, 1:3, :].unsqueeze(2).to_broadcast(shape),
+                in0=y[:, :, :, PLAIN_DIM:HEAD_DIM:2].unsqueeze(4).to_broadcast(shape),
+                in1=first_factors[:, i0 : i0 + GROUP].unsqueeze(2).to_broadcast(shape),
                 op=ALU.mult,
             )
             nc.vector.tensor_tensor(
                 out=from_second[:],
-                in0=y[:, :, :, PLAIN_DIM + 1 : HEAD_DIM : 2].unsqueeze(3).to_broadcast(shape),
-                in1=rows[:, :, 0:2, :].unsqueeze(2).to_broadcast(shape),
+                in0=y[:, :, :, PLAIN_DIM + 1 : HEAD_DIM : 2].unsqueeze(4).to_broadcast(shape),
+                in1=second_factors[:, i0 : i0 + GROUP].unsqueeze(2).to_broadcast(shape),
                 op=ALU.mult,
             )
-            nc.scalar.copy(
-                out=res[:, :, :, 0:PLAIN_DIM].rearrange("p h a d -> p a h d"),
-                in_=y[:, :, :, 0:PLAIN_DIM],
-            )
-            nc.vector.tensor_tensor(
-                out=res[:, :, :, PLAIN_DIM:HEAD_DIM].rearrange("p h a (j e) -> p a h j e", e=2),
-                in0=from_first[:].rearrange("p a h e j -> p a h j e"),
-                in1=from_second[:].rearrange("p a h e j -> p a h j e"),
+            nc.scalar.copy(out=res[:, :, :, 0:PLAIN_DIM], in_=y[:, :, :, 0:PLAIN_DIM])
+            adder = nc.gpsimd if g % 2 == 0 else nc.vector
+            adder.tensor_tensor(
+                out=res[:, :, :, PLAIN_DIM:HEAD_DIM],
+                in0=from_first[:].rearrange("p a h j e -> p a h (j e)"),
+                in1=from_second[:].rearrange("p a h j e -> p a h (j e)"),
                 op=ALU.add,
             )
             if a0 + GROUP == CHUNK:
                 rows_out = out[b].rearrange("h (p i) d -> p h i d", i=TOKENS_PER_PARTITION)
-                nc.gpsimd.dma_start(out=rows_out[:, :, i0 : i0 + CHUNK, :], in_=res_of[c][:])
+                first_row = i0 + GROUP - CHUNK
+                nc.sync.dma_start(out=rows_out[:, :, first_row : first_row + CHUNK, :], in_=res_of[c][:])
 
-        transpose(0)
-        transpose(1)
-        project(0)
-        fill_table()
-        for g in range(2, n_groups):
-            transpose(g)
-            project(g - 1)
-            rotate(g - 2)
-        project(n_groups - 1)
-        rotate(n_groups - 2)
-        rotate(n_groups - 1)
+        for g in range(n_groups + 2 * RUN):
+            if g < n_groups:
+                transpose(g)
+            if g == 1:
+                fill_tables()
+            if g >= 2 * RUN:
+                rotate(g - 2 * RUN)
+            if 1 <= g <= n_groups:
+                quantise(g - 1)
+            if g % RUN == RUN - 1:
+                for m in range(g - 2 * RUN + 1, g - RUN + 1):
+                    if 0 <= m < n_groups:
+                        multiply(m)

@@ -211,8 +211,7 @@ def tile_deepseekv4attention_pb_t_kernel(tc, hidden, wq_words, wq_scales, out):
                 op=ALU.mult,
             )
             nc.scalar.copy(out=res[:, :, :, 0:PLAIN_DIM], in_=y[:, :, :, 0:PLAIN_DIM])
-            adder = nc.gpsimd if g % 2 == 0 else nc.vector
-            adder.tensor_tensor(
+            nc.gpsimd.tensor_tensor(
                 out=res[:, :, :, PLAIN_DIM:HEAD_DIM],
                 in0=from_first[:].rearrange("p a h j e -> p a h (j e)"),
                 in1=from_second[:].rearrange("p a h j e -> p a h (j e)"),

@@ -25,7 +25,10 @@ TOKENS_PER_PARTITION = SEQ // P
 WORDS = HID // 2
 GROUP = 4
 T_BANK = 2
-CHUNK = 8
+HALF = 16
+X_BUFS = 6
+LOAD_PIECES = {0: [2, 2, 2, 2, 8], 1: [8, 8], 2: [8, 8]}
+STORE_PIECES = {0: [32], 1: [32], 2: [16, 16], 3: [16, 8, 4, 4]}
 RUN = 2
 ROUND_MAGIC = 12582912.0
 
@@ -48,10 +51,10 @@ def tile_deepseekv4attention_pb_t_kernel(tc, hidden, wq_words, wq_scales, out):
 
     with ExitStack() as ctx:
         consts = ctx.enter_context(tc.tile_pool(name="consts", bufs=1))
-        x_pool = ctx.enter_context(tc.tile_pool(name="x", bufs=n_groups))
+        x_pool = ctx.enter_context(tc.tile_pool(name="x", bufs=X_BUFS))
         mx_pool = ctx.enter_context(tc.tile_pool(name="mx", bufs=4))
         rope_pool = ctx.enter_context(tc.tile_pool(name="rope", bufs=4))
-        res_pool = ctx.enter_context(tc.tile_pool(name="res", bufs=12))
+        res_pool = ctx.enter_context(tc.tile_pool(name="res", bufs=BATCH))
         t_psum = ctx.enter_context(tc.psum_pool(name="t_psum", bufs=4))
         y_psum = ctx.enter_context(tc.psum_pool(name="y_psum", bufs=4))
         ctx.enter_context(tc.manual_schedule())
@@ -69,14 +72,20 @@ def tile_deepseekv4attention_pb_t_kernel(tc, hidden, wq_words, wq_scales, out):
                 )
 
         x_tiles = []
-        for g, (b, i0) in enumerate(groups):
-            x = x_pool.tile([P, GROUP, HID], BF16)
+
+        def load_half(half):
+            b, i0 = divmod(half * HALF, TOKENS_PER_PARTITION)
+            x = x_pool.tile([P, HALF, HID], BF16, name="x")
             rows = hidden[b].rearrange("(p i) k -> p i k", i=TOKENS_PER_PARTITION)
-            piece = T_BANK if g < RUN else GROUP
-            for a0 in range(0, GROUP, piece):
+            a0 = 0
+            for piece in LOAD_PIECES.get(half, [HALF]):
                 nc.sync.dma_start(out=x[:, a0 : a0 + piece, :], in_=rows[:, i0 + a0 : i0 + a0 + piece, :])
+                a0 += piece
             x_tiles.append(x)
-            if g == 2 * RUN - 1:
+
+        for half in range(X_BUFS):
+            load_half(half)
+            if half == 0:
                 load_w()
 
         position_int = consts.tile([P, TOKENS_PER_PARTITION], I32)
@@ -146,13 +155,14 @@ def tile_deepseekv4attention_pb_t_kernel(tc, hidden, wq_words, wq_scales, out):
         res_of = {}
 
         def transpose(g):
-            x_words = x_tiles[g][:].rearrange("p a k -> p (a k)").bitcast(F32)
+            half, first_tile = divmod(g * GROUP, HALF)
+            x_words = x_tiles[half][:].rearrange("p a k -> p (a k)").bitcast(F32)
             grouped = mx_pool.tile([P, GROUP * P * 4], BF16, align_bytes=64)
             grouped_words = grouped[:].bitcast(F32).rearrange("p (a n u) -> p a n u", n=P, u=2)
             for a0 in range(0, GROUP, T_BANK):
                 flipped = t_psum.tile([P, T_BANK, 2, P], F32)
                 for a in range(T_BANK):
-                    first_word = (a0 + a) * WORDS
+                    first_word = (first_tile + a0 + a) * WORDS
                     for u in range(2):
                         nc.tensor.transpose(
                             flipped[:, a, u, :],
@@ -189,11 +199,9 @@ def tile_deepseekv4attention_pb_t_kernel(tc, hidden, wq_words, wq_scales, out):
 
         def rotate(g):
             b, i0 = groups[g]
-            c = g * GROUP // CHUNK
-            a0 = g * GROUP % CHUNK
-            if a0 == 0:
-                res_of[c] = res_pool.tile([P, HEADS, CHUNK, HEAD_DIM], F32, name="res")
-            res = res_of[c][:, :, a0 : a0 + GROUP, :].rearrange("p h a d -> p a h d")
+            if i0 == 0:
+                res_of[b] = res_pool.tile([P, HEADS, TOKENS_PER_PARTITION, HEAD_DIM], F32, name="res")
+            res = res_of[b][:, :, i0 : i0 + GROUP, :].rearrange("p h a d -> p a h d")
             y = y_of[g][:].rearrange("p a (h d) -> p a h d", h=HEADS)
             from_first = rope_pool.tile([P, GROUP, HEADS, PAIRS, 2], F32)
             from_second = rope_pool.tile([P, GROUP, HEADS, PAIRS, 2], F32)
@@ -217,14 +225,21 @@ def tile_deepseekv4attention_pb_t_kernel(tc, hidden, wq_words, wq_scales, out):
                 in1=from_second[:].rearrange("p a h j e -> p a h (j e)"),
                 op=ALU.add,
             )
-            if a0 + GROUP == CHUNK:
-                rows_out = out[b].rearrange("h (p i) d -> p h i d", i=TOKENS_PER_PARTITION)
-                first_row = i0 + GROUP - CHUNK
-                nc.sync.dma_start(out=rows_out[:, :, first_row : first_row + CHUNK, :], in_=res_of[c][:])
+            first_row = 0
+            for piece in STORE_PIECES[b]:
+                if first_row + piece == i0 + GROUP:
+                    rows_out = out[b].rearrange("h (p i) d -> p h i d", i=TOKENS_PER_PARTITION)
+                    nc.sync.dma_start(
+                        out=rows_out[:, :, first_row : first_row + piece, :],
+                        in_=res_of[b][:, :, first_row : first_row + piece, :],
+                    )
+                first_row += piece
 
         for g in range(n_groups + 2 * RUN):
             if g < n_groups:
                 transpose(g)
+                if (g + 1) * GROUP % HALF == 0 and len(x_tiles) < n_groups * GROUP // HALF:
+                    load_half(len(x_tiles))
             if g == 1:
                 fill_tables()
             if g >= 2 * RUN:

@@ -59,16 +59,38 @@ def tile_deepseekv4attention_pb_t_kernel(tc, hidden, wq_words, wq_scales, out):
         y_psum = ctx.enter_context(tc.psum_pool(name="y_psum", bufs=4))
         ctx.enter_context(tc.manual_schedule())
 
-        w_words = consts.tile([P, 2 * FEATURES], U8, align_bytes=64)
-        w_scales = consts.tile([P, FEATURES], U8, align_bytes=64)
+        w_raw = consts.tile([P, 2 * FEATURES], U8, align_bytes=64)
+        w_split = consts.tile([P, 2, FEATURES], U8, align_bytes=64)
+        w_moved = consts.tile([P, 2, FEATURES], U8, align_bytes=64)
+        w_words = consts.tile([P, 2, 2 * FEATURES], U8, align_bytes=64)
+        w_scales = consts.tile([P, 2, FEATURES], U8, align_bytes=64)
         nc.vector.memset(w_scales[:].bitcast(I32), 0)
+        nc.vector.memset(w_words[:].bitcast(I32), 0)
 
         def load_w():
-            nc.sync.dma_start(out=w_words[:].bitcast(I32), in_=wq_words[0].bitcast(I32))
-            for quadrant in range(4):
-                nc.sync.dma_start(
-                    out=w_scales[32 * quadrant : 32 * quadrant + 4, :].bitcast(I32),
-                    in_=wq_scales[0, 4 * quadrant : 4 * quadrant + 4, :].bitcast(I32),
+            nc.sync.dma_start(out=w_raw[:].bitcast(I32), in_=wq_words[0].bitcast(I32))
+            for u in range(2):
+                for r in range(4):
+                    first_block = 8 * u + r // 2
+                    nc.sync.dma_start(
+                        out=w_scales[r : P : 32, u, :].bitcast(I32),
+                        in_=wq_scales[0, first_block : first_block + 7 : 2, :].bitcast(I32),
+                    )
+
+        def split_w():
+            for e in range(2):
+                nc.vector.tensor_copy(out=w_split[:, e, :], in_=w_raw[:].rearrange("p (n e) -> p e n", e=2)[:, e, :])
+            for u in range(2):
+                for e in range(2):
+                    nc.sync.dma_start(
+                        out=w_moved[e : P : 2, u, :].bitcast(I32),
+                        in_=w_split[64 * u : 64 * u + 64, e, :].bitcast(I32),
+                    )
+
+        def place_w():
+            for u in range(2):
+                nc.vector.tensor_copy(
+                    out=w_words[:, u, :].rearrange("p (n e) -> p e n", e=2)[:, u, :], in_=w_moved[:, u, :]
                 )
 
         x_tiles = []
@@ -83,10 +105,8 @@ def tile_deepseekv4attention_pb_t_kernel(tc, hidden, wq_words, wq_scales, out):
                 a0 += piece
             x_tiles.append(x)
 
-        for half in range(X_BUFS):
-            load_half(half)
-            if half == 0:
-                load_w()
+        load_w()
+        load_half(0)
 
         position_int = consts.tile([P, TOKENS_PER_PARTITION], I32)
         nc.gpsimd.iota(
@@ -116,6 +136,9 @@ def tile_deepseekv4attention_pb_t_kernel(tc, hidden, wq_words, wq_scales, out):
             out=whole[:], in0=turns[:], scalar1=ROUND_MAGIC, scalar2=ROUND_MAGIC, op0=ALU.add, op1=ALU.subtract
         )
         nc.vector.tensor_tensor(out=turns[:], in0=turns[:], in1=whole[:], op=ALU.subtract)
+        split_w()
+        for half in range(1, X_BUFS):
+            load_half(half)
         for j in range(PAIRS):
             nc.vector.scalar_tensor_tensor(
                 out=turns[:, j, :],
@@ -138,6 +161,7 @@ def tile_deepseekv4attention_pb_t_kernel(tc, hidden, wq_words, wq_scales, out):
         nc.vector.tensor_scalar(out=sin_of[:, 0], in0=sin_of[:, 2], scalar1=-1.0, scalar2=None, op0=ALU.mult)
         nc.vector.tensor_tensor(out=sin_of[:, 1], in0=sin_of[:, 0], in1=sin_of[:, 2], op=ALU.min)
         nc.vector.tensor_scalar(out=sin_of[:, 1], in0=sin_of[:, 1], scalar1=0.25, scalar2=None, op0=ALU.add)
+        place_w()
         first_factors = consts.tile([P, TOKENS_PER_PARTITION, PAIRS, 2], F32)
         second_factors = consts.tile([P, TOKENS_PER_PARTITION, PAIRS, 2], F32)
 
@@ -166,7 +190,7 @@ def tile_deepseekv4attention_pb_t_kernel(tc, hidden, wq_words, wq_scales, out):
                     for u in range(2):
                         nc.tensor.transpose(
                             flipped[:, a, u, :],
-                            x_words[:, first_word + u : first_word + WORDS : 2],
+                            x_words[:, first_word + u * P : first_word + (u + 1) * P],
                             identity[:],
                         )
                 nc.scalar.copy(
@@ -186,15 +210,16 @@ def tile_deepseekv4attention_pb_t_kernel(tc, hidden, wq_words, wq_scales, out):
             y = y_psum.tile([P, GROUP, FEATURES], F32)
             for a in range(GROUP):
                 tokens = slice(a * P, (a + 1) * P)
-                nc.tensor.matmul_mx(
-                    out=y[:, a, :],
-                    lhsT=codes[:, tokens].bitcast(FP8X4),
-                    lhsT_scale=scales[:, tokens],
-                    rhs=w_words[:].bitcast(FP4X4),
-                    rhs_scale=w_scales[:],
-                    start=True,
-                    stop=True,
-                )
+                for u in range(2):
+                    nc.tensor.matmul_mx(
+                        out=y[:, a, :],
+                        lhsT=codes[:, tokens].bitcast(FP8X4),
+                        lhsT_scale=scales[:, tokens],
+                        rhs=w_words[:, u, :].bitcast(FP4X4),
+                        rhs_scale=w_scales[:, u, :],
+                        start=(u == 0),
+                        stop=(u == 1),
+                    )
             y_of[g] = y
 
         def rotate(g):

@@ -26,6 +26,7 @@ WORDS = HID // 2
 GROUP = 4
 T_BANK = 2
 HALF = 16
+CHUNK_BEFORE_SCALES = 8
 X_BUFS = 6
 LOAD_PIECES = {0: [2, 2, 2, 2, 8], 1: [8, 8], 2: [8, 8]}
 STORE_PIECES = {0: [32], 1: [32], 2: [16, 16], 3: [16, 8, 4, 4]}
@@ -67,15 +68,10 @@ def tile_deepseekv4attention_pb_t_kernel(tc, hidden, wq_words, wq_scales, out):
         nc.vector.memset(w_scales[:].bitcast(I32), 0)
         nc.vector.memset(w_words[:].bitcast(I32), 0)
 
-        def load_w():
-            nc.sync.dma_start(out=w_raw[:].bitcast(I32), in_=wq_words[0].bitcast(I32))
-            for u in range(2):
-                for r in range(4):
-                    first_block = 8 * u + r // 2
-                    nc.sync.dma_start(
-                        out=w_scales[r : P : 32, u, :].bitcast(I32),
-                        in_=wq_scales[0, first_block : first_block + 7 : 2, :].bitcast(I32),
-                    )
+        def load_w_scales():
+            blocks = wq_scales[0].bitcast(I32).rearrange("(u c h) n -> h c u n", u=2, h=2)
+            for r in range(4):
+                nc.sync.dma_start(out=w_scales[r : P : 32, :, :].bitcast(I32), in_=blocks[r // 2])
 
         def split_w():
             for e in range(2):
@@ -103,9 +99,11 @@ def tile_deepseekv4attention_pb_t_kernel(tc, hidden, wq_words, wq_scales, out):
             for piece in LOAD_PIECES.get(half, [HALF]):
                 nc.sync.dma_start(out=x[:, a0 : a0 + piece, :], in_=rows[:, i0 + a0 : i0 + a0 + piece, :])
                 a0 += piece
+                if half == 0 and a0 == CHUNK_BEFORE_SCALES:
+                    load_w_scales()
             x_tiles.append(x)
 
-        load_w()
+        nc.sync.dma_start(out=w_raw[:].bitcast(I32), in_=wq_words[0].bitcast(I32))
         load_half(0)
 
         position_int = consts.tile([P, TOKENS_PER_PARTITION], I32)
@@ -139,15 +137,10 @@ def tile_deepseekv4attention_pb_t_kernel(tc, hidden, wq_words, wq_scales, out):
         split_w()
         for half in range(1, X_BUFS):
             load_half(half)
+        fine_turns = consts.tile([P, PAIRS, TOKENS_PER_PARTITION], F32)
         for j in range(PAIRS):
-            nc.vector.scalar_tensor_tensor(
-                out=turns[:, j, :],
-                in0=position[:],
-                scalar=splits[j][1],
-                in1=turns[:, j, :],
-                op0=ALU.mult,
-                op1=ALU.add,
-            )
+            nc.scalar.mul(out=fine_turns[:, j, :], in_=position[:], mul=splits[j][1])
+        nc.vector.tensor_tensor(out=turns[:], in0=turns[:], in1=fine_turns[:], op=ALU.add)
         nc.vector.tensor_scalar(
             out=whole[:], in0=turns[:], scalar1=ROUND_MAGIC, scalar2=ROUND_MAGIC, op0=ALU.add, op1=ALU.subtract
         )
@@ -158,10 +151,12 @@ def tile_deepseekv4attention_pb_t_kernel(tc, hidden, wq_words, wq_scales, out):
             in1=whole[:].rearrange("p j i -> p i j"),
             op=ALU.subtract,
         )
-        nc.vector.tensor_scalar(out=sin_of[:, 0], in0=sin_of[:, 2], scalar1=-1.0, scalar2=None, op0=ALU.mult)
-        nc.vector.tensor_tensor(out=sin_of[:, 1], in0=sin_of[:, 0], in1=sin_of[:, 2], op=ALU.min)
-        nc.vector.tensor_scalar(out=sin_of[:, 1], in0=sin_of[:, 1], scalar1=0.25, scalar2=None, op0=ALU.add)
-        place_w()
+
+        def other_arguments():
+            nc.vector.tensor_scalar(out=sin_of[:, 0], in0=sin_of[:, 2], scalar1=-1.0, scalar2=None, op0=ALU.mult)
+            nc.vector.tensor_tensor(out=sin_of[:, 1], in0=sin_of[:, 0], in1=sin_of[:, 2], op=ALU.min)
+            nc.vector.tensor_scalar(out=sin_of[:, 1], in0=sin_of[:, 1], scalar1=0.25, scalar2=None, op0=ALU.add)
+
         first_factors = consts.tile([P, TOKENS_PER_PARTITION, PAIRS, 2], F32)
         second_factors = consts.tile([P, TOKENS_PER_PARTITION, PAIRS, 2], F32)
 
@@ -265,12 +260,15 @@ def tile_deepseekv4attention_pb_t_kernel(tc, hidden, wq_words, wq_scales, out):
                 transpose(g)
                 if (g + 1) * GROUP % HALF == 0 and len(x_tiles) < n_groups * GROUP // HALF:
                     load_half(len(x_tiles))
-            if g == 1:
+            if g == 2 * RUN - 1:
                 fill_tables()
             if g >= 2 * RUN:
                 rotate(g - 2 * RUN)
             if 1 <= g <= n_groups:
                 quantise(g - 1)
+            if g == RUN:
+                place_w()
+                other_arguments()
             if g % RUN == RUN - 1:
                 for m in range(g - 2 * RUN + 1, g - RUN + 1):
                     if 0 <= m < n_groups:

from contextlib import ExitStack

import concourse.mybir as mybir
from concourse.masks import make_identity

F32 = mybir.dt.float32
BF16 = mybir.dt.bfloat16
I32 = mybir.dt.int32
U32 = mybir.dt.uint32
U8 = mybir.dt.uint8
FP8X4 = mybir.dt.float8_e4m3fn_x4
FP4X4 = mybir.dt.float4_e2m1fn_x4
ALU = mybir.AluOpType
SIN = mybir.ActivationFunctionType.Sin

BATCH, SEQ, HID, HEADS, HEAD_DIM, ROPE_DIM = 4, 4096, 512, 2, 64, 32
FEATURES = HEADS * HEAD_DIM
PLAIN_DIM = HEAD_DIM - ROPE_DIM
PAIRS = ROPE_DIM // 2
THETA = 10000.0
TWO_PI = 6.283185307179586

P = 128
TOKENS_PER_PARTITION = SEQ // P
WORDS = HID // 2
GROUP = 4
T_BANK = 2
HALF = 16
CHUNK_BEFORE_SCALES = 8
X_BUFS = 6
LOAD_PIECES = {0: [2, 2, 2, 2, 8], 1: [8, 8], 2: [8, 8]}
STORE_PIECES = {0: [32], 1: [32], 2: [16, 16], 3: [16, 8, 4, 4]}
RUN = 2
ROUND_MAGIC = 12582912.0

FLOPS = 2 * BATCH * SEQ * HID * FEATURES


def split_turns_per_position(j):
    turns = THETA ** (-j / PAIRS) / TWO_PI
    scale = 1.0
    while turns * scale < 2048.0:
        scale *= 2.0
    coarse = round(turns * scale) / scale
    return coarse, turns - coarse


def tile_deepseekv4attention_pb_t_kernel(tc, hidden, wq_words, wq_scales, out):
    nc = tc.nc
    groups = [(b, i0) for b in range(BATCH) for i0 in range(0, TOKENS_PER_PARTITION, GROUP)]
    n_groups = len(groups)

    with ExitStack() as ctx:
        consts = ctx.enter_context(tc.tile_pool(name="consts", bufs=1))
        x_pool = ctx.enter_context(tc.tile_pool(name="x", bufs=X_BUFS))
        mx_pool = ctx.enter_context(tc.tile_pool(name="mx", bufs=4))
        rope_pool = ctx.enter_context(tc.tile_pool(name="rope", bufs=4))
        res_pool = ctx.enter_context(tc.tile_pool(name="res", bufs=BATCH))
        t_psum = ctx.enter_context(tc.psum_pool(name="t_psum", bufs=4))
        y_psum = ctx.enter_context(tc.psum_pool(name="y_psum", bufs=4))
        ctx.enter_context(tc.manual_schedule())

        w_raw = consts.tile([P, 2 * FEATURES], U8, align_bytes=64)
        w_split = consts.tile([P, 2, FEATURES], U8, align_bytes=64)
        w_moved = consts.tile([P, 2, FEATURES], U8, align_bytes=64)
        w_words = consts.tile([P, 2, 2 * FEATURES], U8, align_bytes=64)
        w_scales = consts.tile([P, 2, FEATURES], U8, align_bytes=64)
        nc.vector.memset(w_scales[:].bitcast(I32), 0)
        nc.vector.memset(w_words[:].bitcast(I32), 0)

        def load_w_scales():
            blocks = wq_scales[0].bitcast(I32).rearrange("(u c h) n -> h c u n", u=2, h=2)
            for r in range(4):
                nc.sync.dma_start(out=w_scales[r : P : 32, :, :].bitcast(I32), in_=blocks[r // 2])

        def split_w():
            for e in range(2):
                nc.vector.tensor_copy(out=w_split[:, e, :], in_=w_raw[:].rearrange("p (n e) -> p e n", e=2)[:, e, :])
            for u in range(2):
                for e in range(2):
                    nc.sync.dma_start(
                        out=w_moved[e : P : 2, u, :].bitcast(I32),
                        in_=w_split[64 * u : 64 * u + 64, e, :].bitcast(I32),
                    )

        def place_w():
            for u in range(2):
                nc.vector.tensor_copy(
                    out=w_words[:, u, :].rearrange("p (n e) -> p e n", e=2)[:, u, :], in_=w_moved[:, u, :]
                )

        x_tiles = []

        def load_half(half):
            b, i0 = divmod(half * HALF, TOKENS_PER_PARTITION)
            x = x_pool.tile([P, HALF, HID], BF16, name="x")
            rows = hidden[b].rearrange("(p i) k -> p i k", i=TOKENS_PER_PARTITION)
            a0 = 0
            for piece in LOAD_PIECES.get(half, [HALF]):
                nc.sync.dma_start(out=x[:, a0 : a0 + piece, :], in_=rows[:, i0 + a0 : i0 + a0 + piece, :])
                a0 += piece
                if half == 0 and a0 == CHUNK_BEFORE_SCALES:
                    load_w_scales()
            x_tiles.append(x)

        nc.sync.dma_start(out=w_raw[:].bitcast(I32), in_=wq_words[0].bitcast(I32))
        load_half(0)

        position_int = consts.tile([P, TOKENS_PER_PARTITION], I32)
        nc.gpsimd.iota(
            position_int[:],
            pattern=[[1, TOKENS_PER_PARTITION]],
            base=0,
            channel_multiplier=TOKENS_PER_PARTITION,
        )
        identity = consts.tile([P, P], F32)
        make_identity(nc, identity[:])

        zero = consts.tile([P, 1], F32)
        nc.vector.memset(zero[:], 0.0)
        warm = consts.tile([P, 1], F32)
        nc.scalar.activation(out=warm[:], in_=zero[:], func=SIN)

        position = consts.tile([P, TOKENS_PER_PARTITION], F32)
        nc.vector.tensor_copy(out=position[:], in_=position_int[:])
        splits = [split_turns_per_position(j) for j in range(PAIRS)]
        turns = consts.tile([P, PAIRS, TOKENS_PER_PARTITION], F32)
        whole = consts.tile([P, PAIRS, TOKENS_PER_PARTITION], F32)
        for j in range(PAIRS):
            nc.vector.tensor_scalar(
                out=turns[:, j, :], in0=position[:], scalar1=splits[j][0], scalar2=None, op0=ALU.mult
            )
        nc.vector.tensor_scalar(
            out=whole[:], in0=turns[:], scalar1=ROUND_MAGIC, scalar2=ROUND_MAGIC, op0=ALU.add, op1=ALU.subtract
        )
        nc.vector.tensor_tensor(out=turns[:], in0=turns[:], in1=whole[:], op=ALU.subtract)
        split_w()
        for half in range(1, X_BUFS):
            load_half(half)
        fine_turns = consts.tile([P, PAIRS, TOKENS_PER_PARTITION], F32)
        for j in range(PAIRS):
            nc.scalar.mul(out=fine_turns[:, j, :], in_=position[:], mul=splits[j][1])
        nc.vector.tensor_tensor(out=turns[:], in0=turns[:], in1=fine_turns[:], op=ALU.add)
        nc.vector.tensor_scalar(
            out=whole[:], in0=turns[:], scalar1=ROUND_MAGIC, scalar2=ROUND_MAGIC, op0=ALU.add, op1=ALU.subtract
        )
        sin_of = consts.tile([P, 3, TOKENS_PER_PARTITION, PAIRS], F32)
        nc.vector.tensor_tensor(
            out=sin_of[:, 2],
            in0=turns[:].rearrange("p j i -> p i j"),
            in1=whole[:].rearrange("p j i -> p i j"),
            op=ALU.subtract,
        )

        def other_arguments():
            nc.vector.tensor_scalar(out=sin_of[:, 0], in0=sin_of[:, 2], scalar1=-1.0, scalar2=None, op0=ALU.mult)
            nc.vector.tensor_tensor(out=sin_of[:, 1], in0=sin_of[:, 0], in1=sin_of[:, 2], op=ALU.min)
            nc.vector.tensor_scalar(out=sin_of[:, 1], in0=sin_of[:, 1], scalar1=0.25, scalar2=None, op0=ALU.add)

        first_factors = consts.tile([P, TOKENS_PER_PARTITION, PAIRS, 2], F32)
        second_factors = consts.tile([P, TOKENS_PER_PARTITION, PAIRS, 2], F32)

        def fill_tables():
            nc.scalar.activation(
                out=first_factors[:], in_=sin_of[:, 1:3].rearrange("p e i j -> p i j e"), func=SIN, scale=TWO_PI
            )
            nc.scalar.activation(
                out=second_factors[:], in_=sin_of[:, 0:2].rearrange("p e i j -> p i j e"), func=SIN, scale=TWO_PI
            )

        grouped_of = {}
        mx_of = {}
        y_of = {}
        res_of = {}

        def transpose(g):
            half, first_tile = divmod(g * GROUP, HALF)
            x_words = x_tiles[half][:].rearrange("p a k -> p (a k)").bitcast(F32)
            grouped = mx_pool.tile([P, GROUP * P * 4], BF16, align_bytes=64)
            grouped_words = grouped[:].bitcast(F32).rearrange("p (a n u) -> p a n u", n=P, u=2)
            for a0 in range(0, GROUP, T_BANK):
                flipped = t_psum.tile([P, T_BANK, 2, P], F32)
                for a in range(T_BANK):
                    first_word = (first_tile + a0 + a) * WORDS
                    for u in range(2):
                        nc.tensor.transpose(
                            flipped[:, a, u, :],
                            x_words[:, first_word + u * P : first_word + (u + 1) * P],
                            identity[:],
                        )
                nc.scalar.copy(
                    out=grouped_words[:, a0 : a0 + T_BANK, :, :],
                    in_=flipped[:].rearrange("p a u n -> p a n u"),
                )
            grouped_of[g] = grouped

        def quantise(g):
            codes = mx_pool.tile([P, GROUP * P], U32, align_bytes=64)
            scales = mx_pool.tile([P, GROUP * P], U8, align_bytes=64)
            nc.vector.quantize_mx(out=codes[:].bitcast(FP8X4), scales=scales[:], in_=grouped_of[g][:])
            mx_of[g] = (codes, scales)

        def multiply(g):
            codes, scales = mx_of[g]
            y = y_psum.tile([P, GROUP, FEATURES], F32)
            for a in range(GROUP):
                tokens = slice(a * P, (a + 1) * P)
                for u in range(2):
                    nc.tensor.matmul_mx(
                        out=y[:, a, :],
                        lhsT=codes[:, tokens].bitcast(FP8X4),
                        lhsT_scale=scales[:, tokens],
                        rhs=w_words[:, u, :].bitcast(FP4X4),
                        rhs_scale=w_scales[:, u, :],
                        start=(u == 0),
                        stop=(u == 1),
                    )
            y_of[g] = y

        def rotate(g):
            b, i0 = groups[g]
            if i0 == 0:
                res_of[b] = res_pool.tile([P, HEADS, TOKENS_PER_PARTITION, HEAD_DIM], F32, name="res")
            res = res_of[b][:, :, i0 : i0 + GROUP, :].rearrange("p h a d -> p a h d")
            y = y_of[g][:].rearrange("p a (h d) -> p a h d", h=HEADS)
            from_first = rope_pool.tile([P, GROUP, HEADS, PAIRS, 2], F32)
            from_second = rope_pool.tile([P, GROUP, HEADS, PAIRS, 2], F32)
            shape = [P, GROUP, HEADS, PAIRS, 2]
            nc.vector.tensor_tensor(
                out=from_first[:],
                in0=y[:, :, :, PLAIN_DIM:HEAD_DIM:2].unsqueeze(4).to_broadcast(shape),
                in1=first_factors[:, i0 : i0 + GROUP].unsqueeze(2).to_broadcast(shape),
                op=ALU.mult,
            )
            nc.vector.tensor_tensor(
                out=from_second[:],
                in0=y[:, :, :, PLAIN_DIM + 1 : HEAD_DIM : 2].unsqueeze(4).to_broadcast(shape),
                in1=second_factors[:, i0 : i0 + GROUP].unsqueeze(2).to_broadcast(shape),
                op=ALU.mult,
            )
            nc.scalar.copy(out=res[:, :, :, 0:PLAIN_DIM], in_=y[:, :, :, 0:PLAIN_DIM])
            nc.gpsimd.tensor_tensor(
                out=res[:, :, :, PLAIN_DIM:HEAD_DIM],
                in0=from_first[:].rearrange("p a h j e -> p a h (j e)"),
                in1=from_second[:].rearrange("p a h j e -> p a h (j e)"),
                op=ALU.add,
            )
            first_row = 0
            for piece in STORE_PIECES[b]:
                if first_row + piece == i0 + GROUP:
                    rows_out = out[b].rearrange("h (p i) d -> p h i d", i=TOKENS_PER_PARTITION)
                    nc.sync.dma_start(
                        out=rows_out[:, :, first_row : first_row + piece, :],
                        in_=res_of[b][:, :, first_row : first_row + piece, :],
                    )
                first_row += piece

        for g in range(n_groups + 2 * RUN):
            if g < n_groups:
                transpose(g)
                if (g + 1) * GROUP % HALF == 0 and len(x_tiles) < n_groups * GROUP // HALF:
                    load_half(len(x_tiles))
            if g == 2 * RUN - 1:
                fill_tables()
            if g >= 2 * RUN:
                rotate(g - 2 * RUN)
            if 1 <= g <= n_groups:
                quantise(g - 1)
            if g == RUN:
                place_w()
                other_arguments()
            if g % RUN == RUN - 1:
                for m in range(g - 2 * RUN + 1, g - RUN + 1):
                    if 0 <= m < n_groups:
                        multiply(m)
